import numpy as np
import ml_dtypes


def mxq(x, axis, fmt="e4m3"):
    dtype, down = {"e4m3": (ml_dtypes.float8_e4m3fn, 7), "e5m2": (ml_dtypes.float8_e5m2, 14)}[fmt]
    v = np.moveaxis(np.asarray(x, np.float32).astype(ml_dtypes.bfloat16).astype(np.float64), axis, -1)
    blocks = v.reshape(v.shape[:-1] + (-1, 32))
    amax = np.abs(blocks).max(-1, keepdims=True)
    byte = np.maximum(np.where(amax > 0, np.frexp(amax)[1] - 1 + 127, 0) - down, 1)
    scale = np.exp2(byte - 127.0)
    codes = (blocks / scale).astype(np.float32).astype(dtype).astype(np.float64)
    return np.moveaxis((codes * scale).reshape(v.shape), -1, axis)


WIDE = False


def mx_kscale(k):
    if not WIDE:
        return np.ones(k)
    levels = np.array([30, -30])
    if k % 512:
        return np.exp2(np.random.permutation(np.resize(levels, k // 32))).repeat(32)
    a = np.empty((k // 512, 16))
    for p in range(k // 512):
        a[p, :8] = np.random.permutation(np.resize(levels, 8))
        for g in range(8):
            far = levels[np.abs(levels - a[p, g]) >= 10]
            a[p, g + 8] = far[np.random.randint(len(far))]
    return np.exp2(a.ravel()).repeat(32)


BF16 = ml_dtypes.bfloat16


def bf(x):
    return np.asarray(x, np.float32).astype(BF16)


def f64(x):
    return np.asarray(x).astype(np.float64)


B, S, DIM, H, C, NOPE, ROPE, VDIM = 2, 512, 2048, 8, 512, 64, 128, 128
THETA = 10000.0
EPS = 1e-6


def rope_tables():
    freqs = 1.0 / THETA ** (np.arange(0, ROPE, 2, dtype=np.float64) / ROPE)
    ang = np.outer(np.arange(S, dtype=np.float64), freqs)
    return np.cos(ang), np.sin(ang)


def setup_inputs():
    s = mx_kscale(DIM)
    return {"x": bf(np.random.standard_normal((B, S, DIM)) * s),
            "wkv_a": bf(np.random.standard_normal((C + ROPE, DIM)) / np.sqrt(DIM) / s),
            "kv_norm_w": bf(1.0 + 0.1 * np.random.standard_normal(C))}


def reference(x, wkv_a, kv_norm_w):
    kv = mxq(f64(x), 2, "e5m2") @ mxq(f64(wkv_a), 1, "e4m3").T
    kv_lat, k_raw = kv[..., :C], kv[..., C:]
    cos, sin = rope_tables()
    x0, x1 = k_raw[..., 0::2], k_raw[..., 1::2]
    r0 = x0 * cos - x1 * sin
    r1 = x0 * sin + x1 * cos
    k_pe = np.stack([r0, r1], axis=-1).reshape(B, S, ROPE)
    rms = np.sqrt(np.mean(kv_lat * kv_lat, axis=-1, keepdims=True) + EPS)
    kv_cache = kv_lat / rms * f64(kv_norm_w)
    return kv_cache, k_pe

import math
from contextlib import ExitStack

import concourse.mybir as mybir
from concourse.masks import make_identity

B, S, DIM, C, ROPE = 2, 512, 2048, 512, 128
THETA = 10000.0
EPS = 1e-6
FLOPS = 2 * B * S * DIM * (C + ROPE)

F32 = mybir.dt.float32
BF16 = mybir.dt.bfloat16
I32 = mybir.dt.int32
U32 = mybir.dt.uint32
U8 = mybir.dt.uint8
E5M2X4 = mybir.dt.float8_e5m2_x4
E4M3X4 = mybir.dt.float8_e4m3fn_x4
ALU = mybir.AluOpType
ACT = mybir.ActivationFunctionType

P = 128
K_PASS = 512
PASSES = DIM // K_PASS
QUARTERS = 4
TILES = B * S // P
POS_TILES = S // P
PAIRS = ROPE // 2
T_BANKS = 4
LATENT_BANKS = 3
SLABS = (
    [("x", 0), ("latent", 0), ("x", 1), ("latent", 1), ("latent", 2), ("latent", 3), ("rope", 0)]
    + [("x", i) for i in range(2, TILES)]
)
SIZES = [1, 1, 1, 1, 1, 1, 1, 2, 2, 2]
SPLIT_LOADS = 1
FIRST_SORTED = 5
STEPPED_QUARTERS = 0
SHARED_UNTIL = 2
SCALAR_QUARTERS = 0
COS_ROUND = 1
GAIN_ROUND = 3
RADIX = 8
SORT_FIRST = 1
WARM_ROUND = -1


def tile_simplemla_pa_kernel(tc, x, wkv_a, kv_norm_w, out_0, out_1):
    nc = tc.nc
    x_rows = x.flatten_outer_dims()
    cache_rows = out_0.flatten_outer_dims()
    key_rows = out_1.flatten_outer_dims()

    with ExitStack() as ctx:
        keep = ctx.enter_context(tc.tile_pool(name="keep", bufs=1))
        work = ctx.enter_context(tc.tile_pool(name="work", bufs=3))
        psum = ctx.enter_context(tc.psum_pool(name="psum", bufs=1))
        ctx.enter_context(tc.manual_schedule())

        def source(kind, n):
            if kind == "x":
                return x_rows[n * P : (n + 1) * P, :].rearrange("p (q k) -> p q k", q=QUARTERS)
            if kind == "rope":
                return wkv_a[C : C + ROPE, :].rearrange("p (q k) -> p q k", q=QUARTERS)
            return wkv_a[0:C, n * K_PASS : (n + 1) * K_PASS].rearrange("(q p) k -> p q k", p=P)

        ones = keep.tile([P, P], BF16)
        nc.vector.memset(ones[:], 1.0)
        position = keep.tile([P, POS_TILES, 2], F32)
        nc.gpsimd.iota(position[:, :, 0], [[P, POS_TILES]], base=0, channel_multiplier=1,
                       allow_small_or_imprecise_dtypes=True)
        nc.gpsimd.iota(position[:, :, 1], [[-P, POS_TILES]], base=0, channel_multiplier=-1,
                       allow_small_or_imprecise_dtypes=True)
        gain_row = keep.tile([P, C], BF16)
        nc.gpsimd.memset(gain_row[:].bitcast(U32), 0)
        ident = keep.tile([P, P], F32)
        make_identity(nc, ident[:])

        raw = []
        for s, (kind, n) in enumerate(SLABS):
            pieces = 2 if s < SPLIT_LOADS else 1
            width = QUARTERS // pieces
            parts = []
            for h in range(pieces):
                part = keep.tile([P, width, K_PASS], BF16, name=f"raw{s}_{h}", align_bytes=64)
                nc.sync.dma_start(out=part[:], in_=source(kind, n)[:, h * width : (h + 1) * width, :])
                parts.append(part)
            raw.append(parts)
            if s == 1:
                nc.sync.dma_start(out=gain_row[0:1, :], in_=kv_norm_w.unsqueeze(0))

        fine = keep.tile([P, RADIX], F32)
        for v in range(RADIX):
            nc.vector.tensor_scalar(out=fine[:, v : v + 1], in0=ones[:, 0:1], scalar1=THETA ** (-v / PAIRS),
                                    scalar2=None, op0=ALU.mult)
        coarse = keep.tile([P, POS_TILES, RADIX, 2], F32)
        for c in range(RADIX):
            nc.vector.tensor_scalar(out=coarse[:, :, c, :], in0=position[:],
                                    scalar1=THETA ** (-c * RADIX / PAIRS) / (2.0 * math.pi), scalar2=None, op0=ALU.mult)
        turns = keep.tile([P, POS_TILES * RADIX, RADIX, 2], F32)
        shape = [P, POS_TILES * RADIX, RADIX, 2]
        nc.vector.tensor_tensor(
            out=turns[:],
            in0=coarse[:].rearrange("p a c e -> p (a c) e").unsqueeze(2).to_broadcast(shape),
            in1=fine[:].unsqueeze(1).unsqueeze(3).to_broadcast(shape), op=ALU.mult)
        trig = keep.tile([P, 2, POS_TILES * PAIRS, 2], F32)
        signed_turns = turns[:].rearrange("p m v e -> p (m v e)")
        plain_turns = turns[:].rearrange("p m v e -> p (m v) e")[:, :, 0]
        whole = {}

        def count_turns(w):
            angle, shift = ((plain_turns, 0.25), (signed_turns, 0.0))[w]
            count = keep.tile([P, angle.shape[1]], I32, name=f"whole{w}")
            nc.vector.tensor_scalar(out=count[:], in0=angle, scalar1=shift, scalar2=None, op0=ALU.add)
            whole[w] = count

        def drop_whole_turns(w):
            angle, shift = ((plain_turns, 0.25), (signed_turns, 0.0))[w]
            rest = keep.tile([P, angle.shape[1]], F32, name=f"rest{w}")
            nc.vector.scalar_tensor_tensor(out=rest[:], in0=angle, scalar=shift, in1=whole[w][:],
                                           op0=ALU.add, op1=ALU.subtract)
            whole[w] = rest

        def make_trig(w):
            if w == 0:
                spread = whole[w][:].unsqueeze(2).to_broadcast([P, POS_TILES * PAIRS, 2])
            else:
                spread = whole[w][:].rearrange("p (m e) -> p m e", e=2)
            nc.scalar.activation(out=trig[:, w, :, :], in_=spread, func=ACT.Sin, scale=2.0 * math.pi)

        gain = keep.tile([P, C], F32)

        def spread_gain():
            bank = psum.tile([P, C], F32, tag="rope")
            nc.tensor.matmul(bank[:], lhsT=ones[:], rhs=gain_row[:], start=True, stop=True)
            nc.vector.tensor_copy(out=gain[:], in_=bank[:])

        codes, scales, sorted_words, banks, grouped = {}, {}, {}, {}, {}
        latent, rope, rms, products = {}, {}, {}, {}

        def stepped(s):
            return QUARTERS if s < FIRST_SORTED else STEPPED_QUARTERS

        def sort_words(s, by_scalar):
            first = stepped(s)
            if first == QUARTERS:
                return
            words = raw[s][0][:].rearrange("p q k -> p (q k)").bitcast(F32)
            words = words.rearrange("p (q w u) -> p q u w", q=QUARTERS, u=2)
            if s not in sorted_words:
                ordered = work.tile([P, QUARTERS - first, 2, P], F32, tag="ordered", bufs=4)
                sorted_words[s] = ordered
            split = QUARTERS - SCALAR_QUARTERS
            if by_scalar and split < QUARTERS:
                nc.scalar.copy(out=sorted_words[s][:, split - first :, :, :], in_=words[:, split:, :, :])
            if not by_scalar:
                nc.vector.tensor_copy(out=sorted_words[s][:, : split - first, :, :], in_=words[:, first:split, :, :])

        def transpose(s):
            width = QUARTERS // len(raw[s])
            banks[s] = []
            for half in range(2):
                bank = psum.tile([P, 2, 2, P], F32, tag=f"t{(2 * s + half) % T_BANKS}")
                banks[s].append(bank)
                for q in (2 * half, 2 * half + 1):
                    for u in range(2):
                        if q < stepped(s):
                            words = raw[s][q // width][:, q % width, :].bitcast(F32)[:, u::2]
                        else:
                            words = sorted_words[s][:, q - stepped(s), u, :]
                        nc.tensor.transpose(bank[:, q % 2, u, :], words, ident[:])

        def empty_bank(s, half):
            if half == 0:
                rows = work.tile([P, QUARTERS * K_PASS], BF16, tag="grouped", bufs=4, align_bytes=64)
                grouped[s] = rows
            words = grouped[s][:].bitcast(F32).rearrange("p (q r u) -> p q r u", q=QUARTERS, u=2)
            copy = nc.vector.tensor_copy if half == 1 and s < SHARED_UNTIL else nc.scalar.copy
            copy(out=words[:, 2 * half : 2 * half + 2, :, :], in_=banks[s][half][:].rearrange("p q u r -> p q r u"))

        def quantize(s):
            kind, n = SLABS[s]
            slab_codes = keep.tile([P, QUARTERS * P], U32, name=f"codes{s}", align_bytes=64)
            slab_scales = keep.tile([P, QUARTERS * P], U8, name=f"scales{s}", align_bytes=64)
            nc.vector.quantize_mx(out=slab_codes[:].bitcast(E5M2X4 if kind == "x" else E4M3X4),
                                  scales=slab_scales[:], in_=grouped[s][:])
            codes[kind, n] = slab_codes
            scales[kind, n] = slab_scales

        def one_pass(out, i, g, kind, n, cols):
            mine = slice(g * P, (g + 1) * P)
            nc.tensor.matmul_mx(
                out=out,
                lhsT=codes["x", i][:, mine].bitcast(E5M2X4), lhsT_scale=scales["x", i][:, mine],
                rhs=codes[kind, n][:, cols].bitcast(E4M3X4), rhs_scale=scales[kind, n][:, cols],
                start=(g == 0), stop=(g == PASSES - 1))

        last_banks = [f"t{(2 * (len(SLABS) - 2) + n) % T_BANKS}" for n in range(T_BANKS)]

        def latent_tag(i):
            return f"latent{i % LATENT_BANKS}" if i < TILES - 1 else last_banks[2]

        def key_tag(i):
            return {TILES - 3: last_banks[0], TILES - 2: last_banks[1]}.get(i, "rope")

        def multiply(first, upto):
            old, have = SLABS[:first], SLABS[:upto]
            pairs = [(i, g) for i in range(TILES) for g in range(PASSES)
                     if ("x", i) in have and ("latent", g) in have
                     and not (("x", i) in old and ("latent", g) in old)]
            for i, g in pairs:
                if g == 0:
                    bank = psum.tile([P, C], F32, tag=latent_tag(i))
                    latent[i] = bank
                one_pass(latent[i][:], i, g, "latent", g, slice(0, C))
            keys = [i for i in range(TILES)
                    if ("x", i) in have and ("rope", 0) in have and not (("x", i) in old and ("rope", 0) in old)]
            key_bank = None
            if keys:
                bank = psum.tile([P, len(keys) * ROPE], F32, tag=key_tag(keys[0]))
                key_bank = bank[:]
                for slot, i in enumerate(keys):
                    for g in range(PASSES):
                        one_pass(key_bank[:, slot * ROPE : (slot + 1) * ROPE], i, g, "rope", 0, slice(g * P, (g + 1) * P))
            return [i for i, g in pairs if g == PASSES - 1], keys, key_bank

        def measure(group):
            totals = work.tile([P, len(group)], F32, tag="totals")
            for slot, i in enumerate(group):
                squares = work.tile([P, C], BF16, tag="squares", bufs=2)
                nc.scalar.activation(out=squares[:], in_=latent[i][:], func=ACT.Square,
                                     accum_out=totals[:, slot : slot + 1])
            inverse = work.tile([P, len(group)], F32, tag="inverse")
            nc.scalar.activation(out=inverse[:], in_=totals[:], func=ACT.Abs_reciprocal_sqrt, scale=1.0 / C, bias=EPS)
            return inverse

        def normalise(i, inverse):
            result = work.tile([P, C], F32, tag="cache", bufs=4)
            nc.vector.scalar_tensor_tensor(out=result[:], in0=latent[i][:], scalar=inverse, in1=gain[:],
                                           op0=ALU.mult, op1=ALU.mult)
            nc.sync.dma_start(out=cache_rows[i * P : (i + 1) * P, :], in_=result[:])

        def rope_products(group, bank):
            a = group[0] % POS_TILES
            width = len(group) * ROPE
            both = work.tile([P, 2, width], F32, tag="products", bufs=3)
            factors = trig[:].rearrange("p w m e -> p w (m e)")[:, :, a * ROPE : a * ROPE + width]
            nc.vector.tensor_tensor(out=both[:], in0=bank.unsqueeze(1).to_broadcast([P, 2, width]), in1=factors,
                                    op=ALU.mult)
            return both

        def rope_sum(group, both):
            result = work.tile([P, len(group), ROPE], F32, tag="key")
            pairs = both[:].rearrange("p w (m e) -> p w m e", e=2)
            nc.vector.tensor_tensor(out=result[:].rearrange("p i (j e) -> p (i j) e", e=2),
                                    in0=pairs[:, 0, :, :], in1=pairs[:, 1, :, ::-1], op=ALU.add)
            rows = key_rows[group[0] * P : (group[-1] + 1) * P, :]
            nc.sync.dma_start(out=rows.rearrange("(i p) c -> p i c", p=P), in_=result[:])

        def finish(normed, roots, keys, key_bank):
            runs = [[i for i in keys if i // POS_TILES == b] for b in range(B)]
            runs = [run for run in runs if run]
            both = [rope_products(run, key_bank[:, keys.index(run[0]) * ROPE : (keys.index(run[-1]) + 1) * ROPE])
                    for run in runs]
            early = 0 if TILES - 1 in normed else 1
            for slot, i in enumerate(normed[:early]):
                normalise(i, roots[:, slot : slot + 1])
            for run, prod in zip(runs, both):
                rope_sum(run, prod)
            for slot, i in list(enumerate(normed))[early:]:
                normalise(i, roots[:, slot : slot + 1])

        count_turns(1)
        count_turns(0)
        drop_whole_turns(1)
        drop_whole_turns(0)
        make_trig(1)
        rounds, start = [], 0
        for size in SIZES:
            rounds.append(list(range(start, start + size)))
            start += size
        normed, roots, keys, key_bank = [], None, [], None
        multiplied = 0
        for r, slabs in enumerate(rounds):
            coming = rounds[r + 1] if r + 1 < len(rounds) else []
            for s in slabs:
                transpose(s)
            if len(slabs) == 1 and SORT_FIRST:
                for s in coming:
                    sort_words(s, False)
            if r > 0:
                quantize(slabs[0] - 1)
            finish(normed, roots, keys, key_bank)
            for s in slabs:
                empty_bank(s, 0)
                empty_bank(s, 1)
            if r == COS_ROUND:
                make_trig(0)
            if r == WARM_ROUND:
                warm = keep.tile([P, 1], F32)
                nc.scalar.activation(out=warm[:], in_=ones[:, 0:1], func=ACT.Abs_reciprocal_sqrt)
            if r == GAIN_ROUND:
                spread_gain()
            if not coming:
                break
            upto = max(0, slabs[-1] - 1)
            normed, keys, key_bank = multiply(multiplied, upto)
            multiplied = upto
            for s in slabs[:-1]:
                quantize(s)
            if not (len(slabs) == 1 and SORT_FIRST):
                for s in coming:
                    sort_words(s, False)
            for s in coming:
                sort_words(s, True)
            if normed:
                roots = measure(normed)
        normed, keys = [], []
        waiting = list(rounds[-1])
        for upto in range(multiplied + 1, len(SLABS) + 1):
            before = (normed, roots, keys, key_bank)
            normed, keys, key_bank = multiply(upto - 1, upto)
            if waiting:
                quantize(waiting.pop(0))
            finish(*before)
            roots = measure(normed)
        finish(normed, roots, keys, key_bank)
